import numpy as np
import ml_dtypes


def mxq(x, axis, fmt="e4m3"):
    dtype, down = {"e4m3": (ml_dtypes.float8_e4m3fn, 7), "e5m2": (ml_dtypes.float8_e5m2, 14)}[fmt]
    v = np.moveaxis(np.asarray(x, np.float32).astype(ml_dtypes.bfloat16).astype(np.float64), axis, -1)
    blocks = v.reshape(v.shape[:-1] + (-1, 32))
    amax = np.abs(blocks).max(-1, keepdims=True)
    byte = np.maximum(np.where(amax > 0, np.frexp(amax)[1] - 1 + 127, 0) - down, 1)
    scale = np.exp2(byte - 127.0)
    codes = (blocks / scale).astype(np.float32).astype(dtype).astype(np.float64)
    return np.moveaxis((codes * scale).reshape(v.shape), -1, axis)


WIDE = False


def mx_kscale(k):
    if not WIDE:
        return np.ones(k)
    levels = np.array([20, -20, 10, -10, 0])
    a = np.random.permutation(np.resize(levels, k // 512 * 4)).reshape(k // 512, 4)
    idx = np.arange(k)
    return np.exp2(a[idx // 512, idx % 128 // 32])


BF16 = ml_dtypes.bfloat16


def bf(x):
    return np.asarray(x, np.float32).astype(BF16)


def f64(x):
    return np.asarray(x).astype(np.float64)


B, T, HP, WP, NH, D, DFF = 16, 8, 3, 4, 16, 1024, 4096
HW = HP * WP
N = B * T * HW


def setup_inputs():
    s = mx_kscale(N).reshape(B * T, HW, 1)
    c = np.random.standard_normal((B * T, 1 + HW, D)) * 1.5 / np.sqrt(1 + HW)
    c[:, 0, :] *= 5.0
    c[:, 1:, :] *= s
    x_res = np.random.standard_normal((B, 1 + HW * T, D)) * 1.1
    w = np.random.standard_normal((D, D)) / np.sqrt(D)
    b = 0.1 * np.random.standard_normal(D)
    g = np.random.standard_normal((B, 1 + HW * T, D)) * np.exp2(np.random.randint(-12, 1, (B, 1 + HW * T, 1)))
    g[:, 1:, :] /= s.reshape(B, T, HW, 1).swapaxes(1, 2).reshape(B, HW * T, 1)
    return {"ctx_s": bf(c), "x_res": bf(x_res), "s_out_w": bf(w), "s_out_b": bf(b), "grad_out": bf(g)}


def reference(ctx_s, x_res, s_out_w, s_out_b, grad_out):
    c = f64(ctx_s)
    g = f64(grad_out)
    cp = c[:, 1:, :].reshape(N, D)
    gp = g[:, 1:, :].reshape(B, HW, T, D).swapaxes(1, 2).reshape(N, D)
    dw = mxq(cp, 0, "e4m3").T @ mxq(gp, 0, "e5m2")
    cc = c[:, 0, :].reshape(B, T, D).mean(axis=1)
    return dw + cc.T @ g[:, 0, :]

@@ -1,0 +1,165 @@
+from contextlib import ExitStack
+
+import concourse.mybir as mybir
+
+BF16 = mybir.dt.bfloat16
+F32 = mybir.dt.float32
+U32 = mybir.dt.uint32
+U8 = mybir.dt.uint8
+E4M3_X4 = mybir.dt.float8_e4m3fn_x4
+E5M2_X4 = mybir.dt.float8_e5m2_x4
+
+P = 128
+SLOTS = 4
+BLOCK = 32
+SAMPLES, FRAMES, PATCHES, D = 16, 8, 12, 1024
+PASSES = FRAMES * PATCHES // BLOCK
+M_TILE = 128
+N_TILE = 512
+HALVES = D // N_TILE
+WAVE = 8
+
+FLOPS = 2 * SAMPLES * FRAMES * PATCHES * D * D + 2 * SAMPLES * D * D
+BYTES = 2 * SAMPLES * FRAMES * (PATCHES + 1) * D + 2 * SAMPLES * (FRAMES * PATCHES + 1) * D + 4 * D * D
+
+
+def block_layout(c):
+    spans = []
+    for t in range(FRAMES):
+        first = max(BLOCK * c - PATCHES * t, 0)
+        end = min(BLOCK * (c + 1) - PATCHES * t, PATCHES)
+        if end > first:
+            spans.append((t, first, end))
+    long_spans = [span for span in spans if span[2] - span[1] >= 8]
+    p0 = max(first for t, first, end in long_spans)
+    t0 = long_spans[0][0]
+    fours = []
+    for t, first, end in spans:
+        if end - first == 4:
+            fours.append((t, first))
+        elif end - first == 12:
+            fours.append((t, first if p0 > first else p0 + 8))
+    placed = [(t, p, len(long_spans) + k // 2, k % 2) for k, (t, p) in enumerate(fours)]
+    return (p0, t0, len(long_spans)), placed
+
+
+def regroup(copy, grouped, raw):
+    copy(
+        out=grouped.rearrange("q (c i) j -> q c j i", i=4),
+        in_=raw.rearrange("q j (c i) -> q c j i", i=4),
+    )
+
+
+def tile_timesformerlayer_pc_kernel(tc, ctx_s, x_res, s_out_w, s_out_b, grad_out, out):
+    nc = tc.nc
+    ctx_patch = ctx_s.rearrange("(b t) q w -> b t q w", t=FRAMES)[:, :, 1:, :]
+    grad_patch = grad_out[:, 1:, :].rearrange("b (p t) w -> b p t w", t=FRAMES)
+
+    with ExitStack() as stack:
+        keep = stack.enter_context(tc.tile_pool(name="keep", bufs=1))
+        stage_pool = stack.enter_context(tc.tile_pool(name="stage", bufs=4))
+        psum = stack.enter_context(tc.psum_pool(name="psum", bufs=8))
+
+        ctx_raw = [keep.tile([P, SLOTS, D], BF16, name="ctx_raw%d" % c) for c in range(PASSES)]
+        grad_raw = [keep.tile([P, SLOTS, D], BF16, name="grad_raw%d" % c) for c in range(PASSES)]
+        ctx_cls = keep.tile([P, D], BF16)
+        grad_cls = keep.tile([P, D], BF16)
+        result = [keep.tile([P, D], F32, name="result%d" % m) for m in range(D // M_TILE)]
+
+        ctx_codes = keep.tile([P, PASSES, D], U32, align_bytes=64)
+        ctx_scales = keep.tile([P, PASSES, D], U8, align_bytes=64)
+        grad_codes = keep.tile([P, PASSES, D], U32, align_bytes=64)
+        grad_scales = keep.tile([P, PASSES, D], U8, align_bytes=64)
+
+        def load_grad(c):
+            (p0, t0, whole), fours = block_layout(c)
+            nc.sync.dma_start(
+                out=grad_raw[c][:, 0:whole, :].rearrange("q j w -> q (j w)"),
+                in_=grad_patch[:, p0 : p0 + 8, t0 : t0 + whole, :].rearrange("b p t w -> b p (t w)"),
+            )
+            for t, p, slot, q0 in fours:
+                nc.sync.dma_start(out=grad_raw[c][q0:P:2, slot, :], in_=grad_patch[:, p : p + 4, t, :])
+
+        def load_ctx(c):
+            (p0, t0, whole), fours = block_layout(c)
+            for k in range(whole):
+                nc.sync.dma_start(out=ctx_raw[c][:, k, :], in_=ctx_patch[:, t0 + k, p0 : p0 + 8, :])
+            for t, p, slot, q0 in fours:
+                nc.sync.dma_start(out=ctx_raw[c][q0:P:2, slot, :], in_=ctx_patch[:, t, p : p + 4, :])
+
+        def quantise_piece(copy, raw, codes, scales, fmt, c, half):
+            cols = slice(half * N_TILE, (half + 1) * N_TILE)
+            grouped = stage_pool.tile([P, N_TILE, SLOTS], BF16, align_bytes=64)
+            regroup(copy, grouped[:], raw[c][:, :, cols])
+            nc.vector.quantize_mx(
+                out=codes[:, c, cols].bitcast(fmt),
+                scales=scales[:, c, cols],
+                in_=grouped[:].rearrange("q w j -> q (w j)"),
+            )
+
+        def class_part(m, h):
+            rows = slice(m * M_TILE, (m + 1) * M_TILE)
+            cols = slice(h * N_TILE, (h + 1) * N_TILE)
+            cls = psum.tile([M_TILE, N_TILE], F32, tag="bank")
+            nc.tensor.matmul(out=cls[:], lhsT=ctx_cls[:, rows], rhs=grad_cls[:, cols], start=True, stop=True)
+            nc.scalar.mul(out=result[m][:, cols], in_=cls[:], mul=1.0 / FRAMES)
+
+        def patch_pass(acc, m, h, c):
+            rows = slice(m * M_TILE, (m + 1) * M_TILE)
+            cols = slice(h * N_TILE, (h + 1) * N_TILE)
+            nc.tensor.matmul_mx(
+                out=acc[:],
+                lhsT=ctx_codes[:, c, rows].bitcast(E4M3_X4),
+                lhsT_scale=ctx_scales[:, c, rows],
+                rhs=grad_codes[:, c, cols].bitcast(E5M2_X4),
+                rhs_scale=grad_scales[:, c, cols],
+                start=(c == 0),
+                stop=(c == PASSES - 1),
+            )
+
+        def finish(acc, m, h):
+            rows = slice(m * M_TILE, (m + 1) * M_TILE)
+            cols = slice(h * N_TILE, (h + 1) * N_TILE)
+            nc.vector.tensor_tensor(
+                out=result[m][:, cols], in0=acc[:], in1=result[m][:, cols], op=mybir.AluOpType.add
+            )
+            nc.sync.dma_start(out=out[rows, cols], in_=result[m][:, cols])
+
+        def quantise_grad(copy, c, h):
+            quantise_piece(copy, grad_raw, grad_codes, grad_scales, E5M2_X4, c, h)
+
+        def quantise_ctx(copy, c, s):
+            quantise_piece(copy, ctx_raw, ctx_codes, ctx_scales, E4M3_X4, c, s)
+
+        tiles = [(m, h) for m in range(D // M_TILE) for h in range(HALVES)]
+        first_wave, second_wave = tiles[:WAVE], tiles[WAVE:]
+
+        for c in range(PASSES):
+            load_grad(c)
+            load_ctx(c)
+            if c == 0:
+                nc.sync.dma_start(out=ctx_cls[:], in_=ctx_s[:, 0, :])
+                nc.sync.dma_start(
+                    out=grad_cls[:], in_=grad_out[:, 0, :].unsqueeze(1).to_broadcast([SAMPLES, FRAMES, D])
+                )
+
+        for m, h in tiles:
+            class_part(m, h)
+
+        accs = [psum.tile([M_TILE, N_TILE], F32, tag="bank", name="acc%d_%d" % (m, h)) for m, h in first_wave]
+        for c in range(PASSES):
+            ctx_copy = nc.scalar.copy if c < PASSES - 1 else nc.vector.tensor_copy
+            quantise_grad(nc.vector.tensor_copy, c, 0)
+            quantise_ctx(ctx_copy, c, 0)
+            quantise_grad(nc.vector.tensor_copy, c, 1)
+            for acc, (m, h) in zip(accs, first_wave):
+                patch_pass(acc, m, h, c)
+            quantise_ctx(ctx_copy, c, 1)
+        for acc, (m, h) in zip(accs, first_wave):
+            finish(acc, m, h)
+
+        for m, h in second_wave:
+            acc = psum.tile([M_TILE, N_TILE], F32, tag="bank")
+            for c in range(PASSES):
+                patch_pass(acc, m, h, c)
+            finish(acc, m, h)

@@ -17,7 +17,8 @@ PASSES = FRAMES * PATCHES // BLOCK
 M_TILE = 128
 N_TILE = 512
 HALVES = D // N_TILE
-WAVE = 8
+WAVE = 6
+LAG = 4
 
 FLOPS = 2 * SAMPLES * FRAMES * PATCHES * D * D + 2 * SAMPLES * D * D
 BYTES = 2 * SAMPLES * FRAMES * (PATCHES + 1) * D + 2 * SAMPLES * (FRAMES * PATCHES + 1) * D + 4 * D * D
@@ -57,10 +58,14 @@ def tile_timesformerlayer_pc_kernel(tc, ctx_s, x_res, s_out_w, s_out_b, grad_out
 
     with ExitStack() as stack:
         keep = stack.enter_context(tc.tile_pool(name="keep", bufs=1))
-        stage_pool = stack.enter_context(tc.tile_pool(name="stage", bufs=4))
-        psum = stack.enter_context(tc.psum_pool(name="psum", bufs=8))
+        stage_pool = stack.enter_context(tc.tile_pool(name="stage", bufs=6))
+        acc_pool = stack.enter_context(tc.psum_pool(name="acc", bufs=WAVE))
+        cls_pool = stack.enter_context(tc.psum_pool(name="cls", bufs=8 - WAVE))
 
-        ctx_raw = [keep.tile([P, SLOTS, D], BF16, name="ctx_raw%d" % c) for c in range(PASSES)]
+        ctx_raw = [
+            [keep.tile([P, SLOTS, N_TILE], BF16, name="ctx_raw%d_%d" % (c, s)) for s in range(HALVES)]
+            for c in range(PASSES)
+        ]
         grad_raw = [keep.tile([P, SLOTS, D], BF16, name="grad_raw%d" % c) for c in range(PASSES)]
         ctx_cls = keep.tile([P, D], BF16)
         grad_cls = keep.tile([P, D], BF16)
@@ -80,17 +85,21 @@ def tile_timesformerlayer_pc_kernel(tc, ctx_s, x_res, s_out_w, s_out_b, grad_out
             for t, p, slot, q0 in fours:
                 nc.sync.dma_start(out=grad_raw[c][q0:P:2, slot, :], in_=grad_patch[:, p : p + 4, t, :])
 
-        def load_ctx(c):
+        def load_ctx(c, s):
             (p0, t0, whole), fours = block_layout(c)
+            cols = slice(s * N_TILE, (s + 1) * N_TILE)
             for k in range(whole):
-                nc.sync.dma_start(out=ctx_raw[c][:, k, :], in_=ctx_patch[:, t0 + k, p0 : p0 + 8, :])
+                nc.sync.dma_start(out=ctx_raw[c][s][:, k, :], in_=ctx_patch[:, t0 + k, p0 : p0 + 8, cols])
             for t, p, slot, q0 in fours:
-                nc.sync.dma_start(out=ctx_raw[c][q0:P:2, slot, :], in_=ctx_patch[:, t, p : p + 4, :])
+                nc.sync.dma_start(out=ctx_raw[c][s][q0:P:2, slot, :], in_=ctx_patch[:, t, p : p + 4, cols])
 
-        def quantise_piece(copy, raw, codes, scales, fmt, c, half):
-            cols = slice(half * N_TILE, (half + 1) * N_TILE)
+        def regroup_piece(copy, raw):
             grouped = stage_pool.tile([P, N_TILE, SLOTS], BF16, align_bytes=64)
-            regroup(copy, grouped[:], raw[c][:, :, cols])
+            regroup(copy, grouped[:], raw)
+            return grouped
+
+        def quantise_piece(grouped, codes, scales, fmt, c, half):
+            cols = slice(half * N_TILE, (half + 1) * N_TILE)
             nc.vector.quantize_mx(
                 out=codes[:, c, cols].bitcast(fmt),
                 scales=scales[:, c, cols],
@@ -100,7 +109,7 @@ def tile_timesformerlayer_pc_kernel(tc, ctx_s, x_res, s_out_w, s_out_b, grad_out
         def class_part(m, h):
             rows = slice(m * M_TILE, (m + 1) * M_TILE)
             cols = slice(h * N_TILE, (h + 1) * N_TILE)
-            cls = psum.tile([M_TILE, N_TILE], F32, tag="bank")
+            cls = cls_pool.tile([M_TILE, N_TILE], F32)
             nc.tensor.matmul(out=cls[:], lhsT=ctx_cls[:, rows], rhs=grad_cls[:, cols], start=True, stop=True)
             nc.scalar.mul(out=result[m][:, cols], in_=cls[:], mul=1.0 / FRAMES)
 
@@ -125,41 +134,63 @@ def tile_timesformerlayer_pc_kernel(tc, ctx_s, x_res, s_out_w, s_out_b, grad_out
             )
             nc.sync.dma_start(out=out[rows, cols], in_=result[m][:, cols])
 
-        def quantise_grad(copy, c, h):
-            quantise_piece(copy, grad_raw, grad_codes, grad_scales, E5M2_X4, c, h)
+        def regroup_grad(copy, c, h):
+            return regroup_piece(copy, grad_raw[c][:, :, h * N_TILE : (h + 1) * N_TILE])
 
-        def quantise_ctx(copy, c, s):
-            quantise_piece(copy, ctx_raw, ctx_codes, ctx_scales, E4M3_X4, c, s)
+        def regroup_ctx(copy, c, s):
+            return regroup_piece(copy, ctx_raw[c][s][:])
+
+        def quantise_grad(grouped, c, h):
+            quantise_piece(grouped, grad_codes, grad_scales, E5M2_X4, c, h)
+
+        def quantise_ctx(grouped, c, s):
+            quantise_piece(grouped, ctx_codes, ctx_scales, E4M3_X4, c, s)
 
         tiles = [(m, h) for m in range(D // M_TILE) for h in range(HALVES)]
-        first_wave, second_wave = tiles[:WAVE], tiles[WAVE:]
+
+        def open_tile(k):
+            return acc_pool.tile([M_TILE, N_TILE], F32, tag="acc", name="acc%d" % k)
 
         for c in range(PASSES):
             load_grad(c)
-            load_ctx(c)
+            load_ctx(c, 0)
             if c == 0:
                 nc.sync.dma_start(out=ctx_cls[:], in_=ctx_s[:, 0, :])
                 nc.sync.dma_start(
                     out=grad_cls[:], in_=grad_out[:, 0, :].unsqueeze(1).to_broadcast([SAMPLES, FRAMES, D])
                 )
-
-        for m, h in tiles:
-            class_part(m, h)
-
-        accs = [psum.tile([M_TILE, N_TILE], F32, tag="bank", name="acc%d_%d" % (m, h)) for m, h in first_wave]
         for c in range(PASSES):
-            ctx_copy = nc.scalar.copy if c < PASSES - 1 else nc.vector.tensor_copy
-            quantise_grad(nc.vector.tensor_copy, c, 0)
-            quantise_ctx(ctx_copy, c, 0)
-            quantise_grad(nc.vector.tensor_copy, c, 1)
-            for acc, (m, h) in zip(accs, first_wave):
-                patch_pass(acc, m, h, c)
-            quantise_ctx(ctx_copy, c, 1)
-        for acc, (m, h) in zip(accs, first_wave):
-            finish(acc, m, h)
+            load_ctx(c, 1)
 
-        for m, h in second_wave:
-            acc = psum.tile([M_TILE, N_TILE], F32, tag="bank")
+        stack.enter_context(tc.manual_schedule())
+
+        accs = [open_tile(k) for k in range(WAVE)]
+        for c in range(PASSES):
+            ctx_grouped = regroup_ctx(nc.scalar.copy, c, 0)
+            left = regroup_grad(nc.vector.tensor_copy, c, 0)
+            right = regroup_grad(nc.vector.tensor_copy, c, 1)
+            quantise_grad(left, c, 0)
+            quantise_grad(right, c, 1)
+            quantise_ctx(ctx_grouped, c, 0)
+            for k in range(2 * c, 2 * c + 2):
+                class_part(tiles[k][0], tiles[k][1])
+            for k in range(WAVE):
+                patch_pass(accs[k], tiles[k][0], tiles[k][1], c)
+
+        first = regroup_ctx(nc.scalar.copy, 0, 1)
+        for k in range(WAVE - LAG):
+            finish(accs[k], tiles[k][0], tiles[k][1])
+        second = regroup_ctx(nc.vector.tensor_copy, 1, 1)
+        third = regroup_ctx(nc.vector.tensor_copy, 2, 1)
+        quantise_ctx(first, 0, 1)
+        quantise_ctx(second, 1, 1)
+        quantise_ctx(third, 2, 1)
+
+        for k in range(WAVE, len(tiles)):
+            class_part(tiles[k][0], tiles[k][1])
+            accs.append(open_tile(k))
             for c in range(PASSES):
-                patch_pass(acc, m, h, c)
-            finish(acc, m, h)
+                patch_pass(accs[k], tiles[k][0], tiles[k][1], c)
+            finish(accs[k - LAG], tiles[k - LAG][0], tiles[k - LAG][1])
+        for k in range(len(tiles) - LAG, len(tiles)):
+            finish(accs[k], tiles[k][0], tiles[k][1])

@@ -18,7 +18,7 @@ M_TILE = 128
 N_TILE = 512
 HALVES = D // N_TILE
 WAVE = 6
-LAG = 4
+CLASS_EARLY = 3
 
 FLOPS = 2 * SAMPLES * FRAMES * PATCHES * D * D + 2 * SAMPLES * D * D
 BYTES = 2 * SAMPLES * FRAMES * (PATCHES + 1) * D + 2 * SAMPLES * (FRAMES * PATCHES + 1) * D + 4 * D * D
@@ -58,7 +58,8 @@ def tile_timesformerlayer_pc_kernel(tc, ctx_s, x_res, s_out_w, s_out_b, grad_out
 
     with ExitStack() as stack:
         keep = stack.enter_context(tc.tile_pool(name="keep", bufs=1))
-        stage_pool = stack.enter_context(tc.tile_pool(name="stage", bufs=6))
+        stage_pool = stack.enter_context(tc.tile_pool(name="stage", bufs=11))
+        half_pool = stack.enter_context(tc.tile_pool(name="half", bufs=2))
         acc_pool = stack.enter_context(tc.psum_pool(name="acc", bufs=WAVE))
         cls_pool = stack.enter_context(tc.psum_pool(name="cls", bufs=8 - WAVE))
 
@@ -113,7 +114,7 @@ def tile_timesformerlayer_pc_kernel(tc, ctx_s, x_res, s_out_w, s_out_b, grad_out
             nc.tensor.matmul(out=cls[:], lhsT=ctx_cls[:, rows], rhs=grad_cls[:, cols], start=True, stop=True)
             nc.scalar.mul(out=result[m][:, cols], in_=cls[:], mul=1.0 / FRAMES)
 
-        def patch_pass(acc, m, h, c):
+        def patch_pass(acc, m, h, c, start, stop):
             rows = slice(m * M_TILE, (m + 1) * M_TILE)
             cols = slice(h * N_TILE, (h + 1) * N_TILE)
             nc.tensor.matmul_mx(
@@ -122,8 +123,8 @@ def tile_timesformerlayer_pc_kernel(tc, ctx_s, x_res, s_out_w, s_out_b, grad_out
                 lhsT_scale=ctx_scales[:, c, rows],
                 rhs=grad_codes[:, c, cols].bitcast(E5M2_X4),
                 rhs_scale=grad_scales[:, c, cols],
-                start=(c == 0),
-                stop=(c == PASSES - 1),
+                start=start,
+                stop=stop,
             )
 
         def finish(acc, m, h):
@@ -164,6 +165,37 @@ def tile_timesformerlayer_pc_kernel(tc, ctx_s, x_res, s_out_w, s_out_b, grad_out
 
         stack.enter_context(tc.manual_schedule())
 
+        def passes(k, order):
+            for n, c in enumerate(order):
+                patch_pass(accs[k], tiles[k][0], tiles[k][1], c, n == 0, n == len(order) - 1)
+
+        def one_pass(ks, c, start, stop):
+            for k in ks:
+                patch_pass(accs[k], tiles[k][0], tiles[k][1], c, start, stop)
+
+        def class_of(k):
+            class_part(tiles[k][0], tiles[k][1])
+
+        def done(k):
+            finish(accs[k], tiles[k][0], tiles[k][1])
+
+        def open_next(n):
+            for unused in range(n):
+                accs.append(open_tile(len(accs)))
+
+        def regroup_quarter(copy, c, first):
+            grouped = half_pool.tile([P, N_TILE // 2, SLOTS], BF16, align_bytes=64)
+            regroup(copy, grouped[:], ctx_raw[c][1][:, :, first : first + N_TILE // 2])
+            return grouped
+
+        def quantise_quarter(grouped, c, first):
+            cols = slice(N_TILE + first, N_TILE + first + N_TILE // 2)
+            nc.vector.quantize_mx(
+                out=ctx_codes[:, c, cols].bitcast(E4M3_X4),
+                scales=ctx_scales[:, c, cols],
+                in_=grouped[:].rearrange("q w j -> q (w j)"),
+            )
+
         accs = [open_tile(k) for k in range(WAVE)]
         for c in range(PASSES):
             ctx_grouped = regroup_ctx(nc.scalar.copy, c, 0)
@@ -172,25 +204,49 @@ def tile_timesformerlayer_pc_kernel(tc, ctx_s, x_res, s_out_w, s_out_b, grad_out
             quantise_grad(left, c, 0)
             quantise_grad(right, c, 1)
             quantise_ctx(ctx_grouped, c, 0)
-            for k in range(2 * c, 2 * c + 2):
-                class_part(tiles[k][0], tiles[k][1])
-            for k in range(WAVE):
-                patch_pass(accs[k], tiles[k][0], tiles[k][1], c)
+            for k in range(CLASS_EARLY * c, CLASS_EARLY * (c + 1)):
+                class_of(k)
+            one_pass(range(WAVE), c, c == 0, c == PASSES - 1)
 
-        first = regroup_ctx(nc.scalar.copy, 0, 1)
-        for k in range(WAVE - LAG):
-            finish(accs[k], tiles[k][0], tiles[k][1])
-        second = regroup_ctx(nc.vector.tensor_copy, 1, 1)
-        third = regroup_ctx(nc.vector.tensor_copy, 2, 1)
-        quantise_ctx(first, 0, 1)
-        quantise_ctx(second, 1, 1)
-        quantise_ctx(third, 2, 1)
-
-        for k in range(WAVE, len(tiles)):
-            class_part(tiles[k][0], tiles[k][1])
-            accs.append(open_tile(k))
-            for c in range(PASSES):
-                patch_pass(accs[k], tiles[k][0], tiles[k][1], c)
-            finish(accs[k - LAG], tiles[k - LAG][0], tiles[k - LAG][1])
-        for k in range(len(tiles) - LAG, len(tiles)):
-            finish(accs[k], tiles[k][0], tiles[k][1])
+        x0 = regroup_ctx(nc.scalar.copy, 0, 1)
+        x2a = regroup_quarter(nc.vector.tensor_copy, 2, 0)
+        done(0)
+        done(1)
+        quantise_quarter(x2a, 2, 0)
+        open_next(2)
+        passes(6, [0, 1, 2])
+        passes(7, [0, 1, 2])
+        x1 = regroup_ctx(nc.scalar.copy, 1, 1)
+        for k in range(2, 6):
+            done(k)
+        open_next(4)
+        one_pass(range(8, 12), 2, True, False)
+        x2b = regroup_quarter(nc.scalar.copy, 2, N_TILE // 2)
+        quantise_ctx(x0, 0, 1)
+        one_pass(range(8, 12), 0, False, False)
+        done(6)
+        done(7)
+        open_next(2)
+        one_pass(range(12, 14), 0, True, False)
+        class_of(9)
+        class_of(10)
+        quantise_ctx(x1, 1, 1)
+        one_pass(range(8, 12), 1, False, True)
+        one_pass(range(12, 14), 1, False, False)
+        done(8)
+        quantise_quarter(x2b, 2, N_TILE // 2)
+        class_of(11)
+        one_pass(range(12, 14), 2, False, True)
+        done(9)
+        class_of(12)
+        open_next(1)
+        passes(14, [0, 1, 2])
+        done(10)
+        class_of(13)
+        class_of(14)
+        open_next(1)
+        passes(15, [0, 1, 2])
+        done(11)
+        class_of(15)
+        for k in range(12, 16):
+            done(k)

@@ -79,10 +79,10 @@ def tile_timesformerlayer_pc_kernel(tc, ctx_s, x_res, s_out_w, s_out_b, grad_out
 
         def load_grad(c):
             (p0, t0, whole), fours = block_layout(c)
-            nc.sync.dma_start(
-                out=grad_raw[c][:, 0:whole, :].rearrange("q j w -> q (j w)"),
-                in_=grad_patch[:, p0 : p0 + 8, t0 : t0 + whole, :].rearrange("b p t w -> b p (t w)"),
-            )
+            for h in range(HALVES):
+                cols = slice(h * N_TILE, (h + 1) * N_TILE)
+                for k in range(whole):
+                    nc.sync.dma_start(out=grad_raw[c][:, k, cols], in_=grad_patch[:, p0 : p0 + 8, t0 + k, cols])
             for t, p, slot, q0 in fours:
                 nc.sync.dma_start(out=grad_raw[c][q0:P:2, slot, :], in_=grad_patch[:, p : p + 4, t, :])
 

@@ -112,6 +112,10 @@ def tile_timesformerlayer_pc_kernel(tc, ctx_s, x_res, s_out_w, s_out_b, grad_out
             cols = slice(h * N_TILE, (h + 1) * N_TILE)
             cls = cls_pool.tile([M_TILE, N_TILE], F32)
             nc.tensor.matmul(out=cls[:], lhsT=ctx_cls[:, rows], rhs=grad_cls[:, cols], start=True, stop=True)
+            return cls
+
+        def class_out(cls, m, h):
+            cols = slice(h * N_TILE, (h + 1) * N_TILE)
             nc.scalar.mul(out=result[m][:, cols], in_=cls[:], mul=1.0 / FRAMES)
 
         def patch_pass(acc, m, h, c, start, stop):
@@ -152,14 +156,21 @@ def tile_timesformerlayer_pc_kernel(tc, ctx_s, x_res, s_out_w, s_out_b, grad_out
         def open_tile(k):
             return acc_pool.tile([M_TILE, N_TILE], F32, tag="acc", name="acc%d" % k)
 
+        warm = keep.tile([P, 2], F32)
+        nc.vector.memset(warm[:, 0:1], 0.0)
+        nc.scalar.mul(out=warm[:, 1:2], in_=warm[:, 0:1], mul=1.0 / FRAMES)
+
         for c in range(PASSES):
             load_grad(c)
             load_ctx(c, 0)
             if c == 0:
                 nc.sync.dma_start(out=ctx_cls[:], in_=ctx_s[:, 0, :])
-                nc.sync.dma_start(
-                    out=grad_cls[:], in_=grad_out[:, 0, :].unsqueeze(1).to_broadcast([SAMPLES, FRAMES, D])
-                )
+                for h in range(HALVES):
+                    cols = slice(h * N_TILE, (h + 1) * N_TILE)
+                    nc.sync.dma_start(
+                        out=grad_cls[:, cols],
+                        in_=grad_out[:, 0, cols].unsqueeze(1).to_broadcast([SAMPLES, FRAMES, N_TILE]),
+                    )
         for c in range(PASSES):
             load_ctx(c, 1)
 
@@ -173,8 +184,17 @@ def tile_timesformerlayer_pc_kernel(tc, ctx_s, x_res, s_out_w, s_out_b, grad_out
             for k in ks:
                 patch_pass(accs[k], tiles[k][0], tiles[k][1], c, start, stop)
 
+        products = {}
+
+        def class_mm(k):
+            products[k] = class_part(tiles[k][0], tiles[k][1])
+
+        def class_ev(k):
+            class_out(products[k], tiles[k][0], tiles[k][1])
+
         def class_of(k):
-            class_part(tiles[k][0], tiles[k][1])
+            class_mm(k)
+            class_ev(k)
 
         def done(k):
             finish(accs[k], tiles[k][0], tiles[k][1])
@@ -216,6 +236,8 @@ def tile_timesformerlayer_pc_kernel(tc, ctx_s, x_res, s_out_w, s_out_b, grad_out
         open_next(2)
         passes(6, [0, 1, 2])
         passes(7, [0, 1, 2])
+        class_mm(9)
+        class_mm(10)
         x1 = regroup_ctx(nc.scalar.copy, 1, 1)
         for k in range(2, 6):
             done(k)
@@ -228,25 +250,25 @@ def tile_timesformerlayer_pc_kernel(tc, ctx_s, x_res, s_out_w, s_out_b, grad_out
         done(7)
         open_next(2)
         one_pass(range(12, 14), 0, True, False)
-        class_of(9)
-        class_of(10)
+        class_ev(9)
+        class_ev(10)
+        class_of(11)
+        class_of(12)
         quantise_ctx(x1, 1, 1)
-        one_pass(range(8, 12), 1, False, True)
+        one_pass(range(8, 10), 1, False, True)
+        class_of(13)
+        one_pass(range(10, 12), 1, False, True)
+        class_of(14)
         one_pass(range(12, 14), 1, False, False)
         done(8)
         quantise_quarter(x2b, 2, N_TILE // 2)
-        class_of(11)
         one_pass(range(12, 14), 2, False, True)
+        class_of(15)
         done(9)
-        class_of(12)
         open_next(1)
         passes(14, [0, 1, 2])
         done(10)
-        class_of(13)
-        class_of(14)
         open_next(1)
         passes(15, [0, 1, 2])
-        done(11)
-        class_of(15)
-        for k in range(12, 16):
+        for k in range(11, 16):
             done(k)

@@ -58,7 +58,7 @@ def tile_timesformerlayer_pc_kernel(tc, ctx_s, x_res, s_out_w, s_out_b, grad_out
 
     with ExitStack() as stack:
         keep = stack.enter_context(tc.tile_pool(name="keep", bufs=1))
-        stage_pool = stack.enter_context(tc.tile_pool(name="stage", bufs=11))
+        stage_pool = stack.enter_context(tc.tile_pool(name="stage", bufs=4))
         half_pool = stack.enter_context(tc.tile_pool(name="half", bufs=2))
         acc_pool = stack.enter_context(tc.psum_pool(name="acc", bufs=WAVE))
         cls_pool = stack.enter_context(tc.psum_pool(name="cls", bufs=8 - WAVE))
@@ -138,6 +138,11 @@ def tile_timesformerlayer_pc_kernel(tc, ctx_s, x_res, s_out_w, s_out_b, grad_out
                 out=result[m][:, cols], in0=acc[:], in1=result[m][:, cols], op=mybir.AluOpType.add
             )
             nc.sync.dma_start(out=out[rows, cols], in_=result[m][:, cols])
+
+        def pool_copy(out, in_):
+            nc.gpsimd.tensor_scalar(
+                out=out, in0=in_, scalar1=1.0, scalar2=0.0, op0=mybir.AluOpType.mult, op1=mybir.AluOpType.add
+            )
 
         def regroup_grad(copy, c, h):
             return regroup_piece(copy, grad_raw[c][:, :, h * N_TILE : (h + 1) * N_TILE])
@@ -229,41 +234,39 @@ def tile_timesformerlayer_pc_kernel(tc, ctx_s, x_res, s_out_w, s_out_b, grad_out
             one_pass(range(WAVE), c, c == 0, c == PASSES - 1)
 
         x0 = regroup_ctx(nc.scalar.copy, 0, 1)
-        x2a = regroup_quarter(nc.vector.tensor_copy, 2, 0)
-        done(0)
-        done(1)
-        quantise_quarter(x2a, 2, 0)
+        x1 = stage_pool.tile([P, N_TILE, SLOTS], BF16, align_bytes=64, name="grouped")
+        pool_copy(out=x1[:], in_=ctx_raw[1][1][:].rearrange("q j w -> q w j"))
+        x2 = regroup_ctx(nc.scalar.copy, 2, 1)
+        for k in range(0, 3):
+            done(k)
         open_next(2)
         passes(6, [0, 1, 2])
         passes(7, [0, 1, 2])
         class_mm(9)
         class_mm(10)
-        x1 = regroup_ctx(nc.scalar.copy, 1, 1)
-        for k in range(2, 6):
+        quantise_ctx(x0, 0, 1)
+        for k in range(3, 6):
             done(k)
         open_next(4)
-        one_pass(range(8, 12), 2, True, False)
-        x2b = regroup_quarter(nc.scalar.copy, 2, N_TILE // 2)
-        quantise_ctx(x0, 0, 1)
-        one_pass(range(8, 12), 0, False, False)
+        one_pass(range(8, 12), 0, True, False)
+        class_ev(9)
+        class_ev(10)
+        quantise_ctx(x1, 1, 1)
+        class_of(11)
+        one_pass(range(8, 12), 1, False, False)
+        quantise_ctx(x2, 2, 1)
+        class_of(12)
+        one_pass(range(8, 10), 2, False, True)
+        class_of(13)
+        one_pass(range(10, 12), 2, False, True)
         done(6)
         done(7)
         open_next(2)
-        one_pass(range(12, 14), 0, True, False)
-        class_ev(9)
-        class_ev(10)
-        class_of(11)
-        class_of(12)
-        quantise_ctx(x1, 1, 1)
-        one_pass(range(8, 10), 1, False, True)
-        class_of(13)
-        one_pass(range(10, 12), 1, False, True)
         class_of(14)
-        one_pass(range(12, 14), 1, False, False)
+        passes(12, [0, 1, 2])
         done(8)
-        quantise_quarter(x2b, 2, N_TILE // 2)
-        one_pass(range(12, 14), 2, False, True)
         class_of(15)
+        passes(13, [0, 1, 2])
         done(9)
         open_next(1)
         passes(14, [0, 1, 2])

@@ -18,7 +18,7 @@ M_TILE = 128
 N_TILE = 512
 HALVES = D // N_TILE
 WAVE = 6
-CLASS_EARLY = 3
+CLASS_EARLY = [4, 3, 2]
 
 FLOPS = 2 * SAMPLES * FRAMES * PATCHES * D * D + 2 * SAMPLES * D * D
 BYTES = 2 * SAMPLES * FRAMES * (PATCHES + 1) * D + 2 * SAMPLES * (FRAMES * PATCHES + 1) * D + 4 * D * D
@@ -229,7 +229,7 @@ def tile_timesformerlayer_pc_kernel(tc, ctx_s, x_res, s_out_w, s_out_b, grad_out
             quantise_grad(left, c, 0)
             quantise_grad(right, c, 1)
             quantise_ctx(ctx_grouped, c, 0)
-            for k in range(CLASS_EARLY * c, CLASS_EARLY * (c + 1)):
+            for k in range(sum(CLASS_EARLY[0:c]), sum(CLASS_EARLY[0 : c + 1])):
                 class_of(k)
             one_pass(range(WAVE), c, c == 0, c == PASSES - 1)
 

@@ -58,8 +58,9 @@ def tile_timesformerlayer_pc_kernel(tc, ctx_s, x_res, s_out_w, s_out_b, grad_out
 
     with ExitStack() as stack:
         keep = stack.enter_context(tc.tile_pool(name="keep", bufs=1))
-        stage_pool = stack.enter_context(tc.tile_pool(name="stage", bufs=4))
-        half_pool = stack.enter_context(tc.tile_pool(name="half", bufs=2))
+        stage_pool = stack.enter_context(tc.tile_pool(name="stage", bufs=3))
+        late_pool = stack.enter_context(tc.tile_pool(name="late", bufs=1))
+        spare_pool = stack.enter_context(tc.tile_pool(name="spare", bufs=2))
         acc_pool = stack.enter_context(tc.psum_pool(name="acc", bufs=WAVE))
         cls_pool = stack.enter_context(tc.psum_pool(name="cls", bufs=8 - WAVE))
 
@@ -208,11 +209,6 @@ def tile_timesformerlayer_pc_kernel(tc, ctx_s, x_res, s_out_w, s_out_b, grad_out
             for unused in range(n):
                 accs.append(open_tile(len(accs)))
 
-        def regroup_quarter(copy, c, first):
-            grouped = half_pool.tile([P, N_TILE // 2, SLOTS], BF16, align_bytes=64)
-            regroup(copy, grouped[:], ctx_raw[c][1][:, :, first : first + N_TILE // 2])
-            return grouped
-
         def quantise_quarter(grouped, c, first):
             cols = slice(N_TILE + first, N_TILE + first + N_TILE // 2)
             nc.vector.quantize_mx(
@@ -220,6 +216,24 @@ def tile_timesformerlayer_pc_kernel(tc, ctx_s, x_res, s_out_w, s_out_b, grad_out
                 scales=ctx_scales[:, c, cols],
                 in_=grouped[:].rearrange("q w j -> q (w j)"),
             )
+
+        def empty_beside(k):
+            patch_sum = spare_pool.tile([M_TILE, N_TILE], F32)
+            nc.scalar.copy(out=patch_sum[:], in_=accs[k][:])
+            return patch_sum
+
+        def add_beside(patch_sum, k):
+            m, h = tiles[k]
+            cols = slice(h * N_TILE, (h + 1) * N_TILE)
+            nc.gpsimd.tensor_tensor(
+                out=result[m][:, cols], in0=patch_sum[:], in1=result[m][:, cols], op=mybir.AluOpType.add
+            )
+
+        def store(k):
+            m, h = tiles[k]
+            rows = slice(m * M_TILE, (m + 1) * M_TILE)
+            cols = slice(h * N_TILE, (h + 1) * N_TILE)
+            nc.sync.dma_start(out=out[rows, cols], in_=result[m][:, cols])
 
         accs = [open_tile(k) for k in range(WAVE)]
         for c in range(PASSES):
@@ -233,10 +247,13 @@ def tile_timesformerlayer_pc_kernel(tc, ctx_s, x_res, s_out_w, s_out_b, grad_out
                 class_of(k)
             one_pass(range(WAVE), c, c == 0, c == PASSES - 1)
 
-        x0 = regroup_ctx(nc.scalar.copy, 0, 1)
+        HALF = N_TILE // 2
+        x0 = late_pool.tile([P, N_TILE, SLOTS], BF16, align_bytes=64, name="late")
+        regroup(nc.scalar.copy, x0[:], ctx_raw[0][1][:])
         x1 = stage_pool.tile([P, N_TILE, SLOTS], BF16, align_bytes=64, name="grouped")
         pool_copy(out=x1[:], in_=ctx_raw[1][1][:].rearrange("q j w -> q w j"))
-        x2 = regroup_ctx(nc.scalar.copy, 2, 1)
+        x2a = stage_pool.tile([P, HALF, SLOTS], BF16, align_bytes=64, name="grouped")
+        regroup(nc.scalar.copy, x2a[:], ctx_raw[2][1][:, :, 0:HALF])
         for k in range(0, 3):
             done(k)
         open_next(2)
@@ -245,24 +262,32 @@ def tile_timesformerlayer_pc_kernel(tc, ctx_s, x_res, s_out_w, s_out_b, grad_out
         class_mm(9)
         class_mm(10)
         quantise_ctx(x0, 0, 1)
+        x2b = late_pool.tile([P, HALF, SLOTS], BF16, align_bytes=64, name="late")
+        pool_copy(out=x2b[:], in_=ctx_raw[2][1][:, :, HALF:N_TILE].rearrange("q j w -> q w j"))
+        class_ev(9)
+        class_ev(10)
         for k in range(3, 6):
             done(k)
         open_next(4)
-        one_pass(range(8, 12), 0, True, False)
-        class_ev(9)
-        class_ev(10)
-        quantise_ctx(x1, 1, 1)
+        one_pass(range(8, 10), 0, True, False)
         class_of(11)
-        one_pass(range(8, 12), 1, False, False)
-        quantise_ctx(x2, 2, 1)
+        one_pass(range(10, 11), 0, True, False)
         class_of(12)
-        one_pass(range(8, 10), 2, False, True)
+        one_pass(range(11, 12), 0, True, False)
         class_of(13)
-        one_pass(range(10, 12), 2, False, True)
+        quantise_ctx(x1, 1, 1)
+        one_pass(range(8, 12), 1, False, False)
+        quantise_quarter(x2a, 2, 0)
+        one_pass(range(8, 12), 2, False, True)
+        quantise_quarter(x2b, 2, HALF)
+        s10 = empty_beside(10)
+        add_beside(s10, 10)
+        s11 = empty_beside(11)
+        add_beside(s11, 11)
+        class_of(14)
         done(6)
         done(7)
         open_next(2)
-        class_of(14)
         passes(12, [0, 1, 2])
         done(8)
         class_of(15)
@@ -270,8 +295,11 @@ def tile_timesformerlayer_pc_kernel(tc, ctx_s, x_res, s_out_w, s_out_b, grad_out
         done(9)
         open_next(1)
         passes(14, [0, 1, 2])
-        done(10)
+        store(10)
+        done(12)
         open_next(1)
         passes(15, [0, 1, 2])
-        for k in range(11, 16):
-            done(k)
+        store(11)
+        done(13)
+        done(14)
+        done(15)

@@ -207,7 +207,7 @@ def tile_timesformerlayer_pc_kernel(tc, ctx_s, x_res, s_out_w, s_out_b, grad_out
 
         def open_next(n):
             for unused in range(n):
-                accs.append(open_tile(len(accs)))
+                accs[len(accs)] = open_tile(len(accs))
 
         def quantise_quarter(grouped, c, first):
             cols = slice(N_TILE + first, N_TILE + first + N_TILE // 2)
@@ -235,17 +235,25 @@ def tile_timesformerlayer_pc_kernel(tc, ctx_s, x_res, s_out_w, s_out_b, grad_out
             cols = slice(h * N_TILE, (h + 1) * N_TILE)
             nc.sync.dma_start(out=out[rows, cols], in_=result[m][:, cols])
 
-        accs = [open_tile(k) for k in range(WAVE)]
+        accs = {}
+        for k in (0, 2, 4, 1, 3, 5):
+            accs[k] = open_tile(k)
         for c in range(PASSES):
             ctx_grouped = regroup_ctx(nc.scalar.copy, c, 0)
             left = regroup_grad(nc.vector.tensor_copy, c, 0)
             right = regroup_grad(nc.vector.tensor_copy, c, 1)
             quantise_grad(left, c, 0)
-            quantise_grad(right, c, 1)
+            if c < PASSES - 1:
+                quantise_grad(right, c, 1)
             quantise_ctx(ctx_grouped, c, 0)
             for k in range(sum(CLASS_EARLY[0:c]), sum(CLASS_EARLY[0 : c + 1])):
                 class_of(k)
-            one_pass(range(WAVE), c, c == 0, c == PASSES - 1)
+            if c < PASSES - 1:
+                one_pass(range(WAVE), c, c == 0, False)
+            else:
+                one_pass(range(0, WAVE, HALVES), c, False, True)
+                quantise_grad(right, c, 1)
+                one_pass(range(1, WAVE, HALVES), c, False, True)
 
         HALF = N_TILE // 2
         x0 = late_pool.tile([P, N_TILE, SLOTS], BF16, align_bytes=64, name="late")
@@ -254,19 +262,20 @@ def tile_timesformerlayer_pc_kernel(tc, ctx_s, x_res, s_out_w, s_out_b, grad_out
         pool_copy(out=x1[:], in_=ctx_raw[1][1][:].rearrange("q j w -> q w j"))
         x2a = stage_pool.tile([P, HALF, SLOTS], BF16, align_bytes=64, name="grouped")
         regroup(nc.scalar.copy, x2a[:], ctx_raw[2][1][:, :, 0:HALF])
-        for k in range(0, 3):
+        for k in (0, 2, 4):
             done(k)
         open_next(2)
         passes(6, [0, 1, 2])
         passes(7, [0, 1, 2])
         class_mm(9)
         class_mm(10)
+        done(1)
         quantise_ctx(x0, 0, 1)
         x2b = late_pool.tile([P, HALF, SLOTS], BF16, align_bytes=64, name="late")
         pool_copy(out=x2b[:], in_=ctx_raw[2][1][:, :, HALF:N_TILE].rearrange("q j w -> q w j"))
         class_ev(9)
         class_ev(10)
-        for k in range(3, 6):
+        for k in (3, 5):
             done(k)
         open_next(4)
         one_pass(range(8, 10), 0, True, False)

@@ -166,6 +166,12 @@ def tile_timesformerlayer_pc_kernel(tc, ctx_s, x_res, s_out_w, s_out_b, grad_out
         nc.vector.memset(warm[:, 0:1], 0.0)
         nc.scalar.mul(out=warm[:, 1:2], in_=warm[:, 0:1], mul=1.0 / FRAMES)
 
+        for engines in (4, 12):
+            nudge = keep.tile([P, 2 * D], BF16, name="nudge%d" % engines)
+            nc.scalar.dma_start(
+                out=nudge[0 : 4 * engines : 4, :], in_=ctx_s[0:engines, 0:2, :].rearrange("s q w -> s (q w)")
+            )
+
         for c in range(PASSES):
             load_grad(c)
             load_ctx(c, 0)

@@ -73,10 +73,10 @@ def tile_timesformerlayer_pc_kernel(tc, ctx_s, x_res, s_out_w, s_out_b, grad_out
         grad_cls = keep.tile([P, D], BF16)
         result = [keep.tile([P, D], F32, name="result%d" % m) for m in range(D // M_TILE)]
 
-        ctx_codes = keep.tile([P, PASSES, D], U32, align_bytes=64)
-        ctx_scales = keep.tile([P, PASSES, D], U8, align_bytes=64)
-        grad_codes = keep.tile([P, PASSES, D], U32, align_bytes=64)
-        grad_scales = keep.tile([P, PASSES, D], U8, align_bytes=64)
+        ctx_codes = keep.tile([P, PASSES, D], U32, align_bytes=256)
+        ctx_scales = keep.tile([P, PASSES, D], U8, align_bytes=256)
+        grad_codes = keep.tile([P, PASSES, D], U32, align_bytes=256)
+        grad_scales = keep.tile([P, PASSES, D], U8, align_bytes=256)
 
         def load_grad(c):
             (p0, t0, whole), fours = block_layout(c)

@@ -166,11 +166,8 @@ def tile_timesformerlayer_pc_kernel(tc, ctx_s, x_res, s_out_w, s_out_b, grad_out
         nc.vector.memset(warm[:, 0:1], 0.0)
         nc.scalar.mul(out=warm[:, 1:2], in_=warm[:, 0:1], mul=1.0 / FRAMES)
 
-        for engines in (4, 12):
-            nudge = keep.tile([P, 2 * D], BF16, name="nudge%d" % engines)
-            nc.scalar.dma_start(
-                out=nudge[0 : 4 * engines : 4, :], in_=ctx_s[0:engines, 0:2, :].rearrange("s q w -> s (q w)")
-            )
+        nudge = keep.tile([P, 2 * D], BF16)
+        nc.scalar.dma_start(out=nudge[0:16:4, :], in_=ctx_s[0:4, 0:2, :].rearrange("s q w -> s (q w)"))
 
         for c in range(PASSES):
             load_grad(c)

from contextlib import ExitStack

import concourse.mybir as mybir

BF16 = mybir.dt.bfloat16
F32 = mybir.dt.float32
U32 = mybir.dt.uint32
U8 = mybir.dt.uint8
E4M3_X4 = mybir.dt.float8_e4m3fn_x4
E5M2_X4 = mybir.dt.float8_e5m2_x4

P = 128
SLOTS = 4
BLOCK = 32
SAMPLES, FRAMES, PATCHES, D = 16, 8, 12, 1024
PASSES = FRAMES * PATCHES // BLOCK
M_TILE = 128
N_TILE = 512
HALVES = D // N_TILE
WAVE = 6
CLASS_EARLY = [4, 3, 2]

FLOPS = 2 * SAMPLES * FRAMES * PATCHES * D * D + 2 * SAMPLES * D * D
BYTES = 2 * SAMPLES * FRAMES * (PATCHES + 1) * D + 2 * SAMPLES * (FRAMES * PATCHES + 1) * D + 4 * D * D


def block_layout(c):
    spans = []
    for t in range(FRAMES):
        first = max(BLOCK * c - PATCHES * t, 0)
        end = min(BLOCK * (c + 1) - PATCHES * t, PATCHES)
        if end > first:
            spans.append((t, first, end))
    long_spans = [span for span in spans if span[2] - span[1] >= 8]
    p0 = max(first for t, first, end in long_spans)
    t0 = long_spans[0][0]
    fours = []
    for t, first, end in spans:
        if end - first == 4:
            fours.append((t, first))
        elif end - first == 12:
            fours.append((t, first if p0 > first else p0 + 8))
    placed = [(t, p, len(long_spans) + k // 2, k % 2) for k, (t, p) in enumerate(fours)]
    return (p0, t0, len(long_spans)), placed


def regroup(copy, grouped, raw):
    copy(
        out=grouped.rearrange("q (c i) j -> q c j i", i=4),
        in_=raw.rearrange("q j (c i) -> q c j i", i=4),
    )


def tile_timesformerlayer_pc_kernel(tc, ctx_s, x_res, s_out_w, s_out_b, grad_out, out):
    nc = tc.nc
    ctx_patch = ctx_s.rearrange("(b t) q w -> b t q w", t=FRAMES)[:, :, 1:, :]
    grad_patch = grad_out[:, 1:, :].rearrange("b (p t) w -> b p t w", t=FRAMES)

    with ExitStack() as stack:
        keep = stack.enter_context(tc.tile_pool(name="keep", bufs=1))
        stage_pool = stack.enter_context(tc.tile_pool(name="stage", bufs=3))
        late_pool = stack.enter_context(tc.tile_pool(name="late", bufs=1))
        spare_pool = stack.enter_context(tc.tile_pool(name="spare", bufs=2))
        acc_pool = stack.enter_context(tc.psum_pool(name="acc", bufs=WAVE))
        cls_pool = stack.enter_context(tc.psum_pool(name="cls", bufs=8 - WAVE))

        ctx_raw = [
            [keep.tile([P, SLOTS, N_TILE], BF16, name="ctx_raw%d_%d" % (c, s)) for s in range(HALVES)]
            for c in range(PASSES)
        ]
        grad_raw = [keep.tile([P, SLOTS, D], BF16, name="grad_raw%d" % c) for c in range(PASSES)]
        ctx_cls = keep.tile([P, D], BF16)
        grad_cls = keep.tile([P, D], BF16)
        result = [keep.tile([P, D], F32, name="result%d" % m) for m in range(D // M_TILE)]

        ctx_codes = keep.tile([P, PASSES, D], U32, align_bytes=256)
        ctx_scales = keep.tile([P, PASSES, D], U8, align_bytes=256)
        grad_codes = keep.tile([P, PASSES, D], U32, align_bytes=256)
        grad_scales = keep.tile([P, PASSES, D], U8, align_bytes=256)

        def load_grad(c):
            (p0, t0, whole), fours = block_layout(c)
            for h in range(HALVES):
                cols = slice(h * N_TILE, (h + 1) * N_TILE)
                for k in range(whole):
                    nc.sync.dma_start(out=grad_raw[c][:, k, cols], in_=grad_patch[:, p0 : p0 + 8, t0 + k, cols])
            for t, p, slot, q0 in fours:
                nc.sync.dma_start(out=grad_raw[c][q0:P:2, slot, :], in_=grad_patch[:, p : p + 4, t, :])

        def load_ctx(c, s):
            (p0, t0, whole), fours = block_layout(c)
            cols = slice(s * N_TILE, (s + 1) * N_TILE)
            for k in range(whole):
                nc.sync.dma_start(out=ctx_raw[c][s][:, k, :], in_=ctx_patch[:, t0 + k, p0 : p0 + 8, cols])
            for t, p, slot, q0 in fours:
                nc.sync.dma_start(out=ctx_raw[c][s][q0:P:2, slot, :], in_=ctx_patch[:, t, p : p + 4, cols])

        def regroup_piece(copy, raw):
            grouped = stage_pool.tile([P, N_TILE, SLOTS], BF16, align_bytes=64)
            regroup(copy, grouped[:], raw)
            return grouped

        def quantise_piece(grouped, codes, scales, fmt, c, half):
            cols = slice(half * N_TILE, (half + 1) * N_TILE)
            nc.vector.quantize_mx(
                out=codes[:, c, cols].bitcast(fmt),
                scales=scales[:, c, cols],
                in_=grouped[:].rearrange("q w j -> q (w j)"),
            )

        def class_part(m, h):
            rows = slice(m * M_TILE, (m + 1) * M_TILE)
            cols = slice(h * N_TILE, (h + 1) * N_TILE)
            cls = cls_pool.tile([M_TILE, N_TILE], F32)
            nc.tensor.matmul(out=cls[:], lhsT=ctx_cls[:, rows], rhs=grad_cls[:, cols], start=True, stop=True)
            return cls

        def class_out(cls, m, h):
            cols = slice(h * N_TILE, (h + 1) * N_TILE)
            nc.scalar.mul(out=result[m][:, cols], in_=cls[:], mul=1.0 / FRAMES)

        def patch_pass(acc, m, h, c, start, stop):
            rows = slice(m * M_TILE, (m + 1) * M_TILE)
            cols = slice(h * N_TILE, (h + 1) * N_TILE)
            nc.tensor.matmul_mx(
                out=acc[:],
                lhsT=ctx_codes[:, c, rows].bitcast(E4M3_X4),
                lhsT_scale=ctx_scales[:, c, rows],
                rhs=grad_codes[:, c, cols].bitcast(E5M2_X4),
                rhs_scale=grad_scales[:, c, cols],
                start=start,
                stop=stop,
            )

        def finish(acc, m, h):
            rows = slice(m * M_TILE, (m + 1) * M_TILE)
            cols = slice(h * N_TILE, (h + 1) * N_TILE)
            nc.vector.tensor_tensor(
                out=result[m][:, cols], in0=acc[:], in1=result[m][:, cols], op=mybir.AluOpType.add
            )
            nc.sync.dma_start(out=out[rows, cols], in_=result[m][:, cols])

        def pool_copy(out, in_):
            nc.gpsimd.tensor_scalar(
                out=out, in0=in_, scalar1=1.0, scalar2=0.0, op0=mybir.AluOpType.mult, op1=mybir.AluOpType.add
            )

        def regroup_grad(copy, c, h):
            return regroup_piece(copy, grad_raw[c][:, :, h * N_TILE : (h + 1) * N_TILE])

        def regroup_ctx(copy, c, s):
            return regroup_piece(copy, ctx_raw[c][s][:])

        def quantise_grad(grouped, c, h):
            quantise_piece(grouped, grad_codes, grad_scales, E5M2_X4, c, h)

        def quantise_ctx(grouped, c, s):
            quantise_piece(grouped, ctx_codes, ctx_scales, E4M3_X4, c, s)

        tiles = [(m, h) for m in range(D // M_TILE) for h in range(HALVES)]

        def open_tile(k):
            return acc_pool.tile([M_TILE, N_TILE], F32, tag="acc", name="acc%d" % k)

        warm = keep.tile([P, 2], F32)
        nc.vector.memset(warm[:, 0:1], 0.0)
        nc.scalar.mul(out=warm[:, 1:2], in_=warm[:, 0:1], mul=1.0 / FRAMES)

        nudge = keep.tile([P, 2 * D], BF16)
        nc.scalar.dma_start(out=nudge[0:16:4, :], in_=ctx_s[0:4, 0:2, :].rearrange("s q w -> s (q w)"))

        for c in range(PASSES):
            load_grad(c)
            load_ctx(c, 0)
            if c == 0:
                nc.sync.dma_start(out=ctx_cls[:], in_=ctx_s[:, 0, :])
                for h in range(HALVES):
                    cols = slice(h * N_TILE, (h + 1) * N_TILE)
                    nc.sync.dma_start(
                        out=grad_cls[:, cols],
                        in_=grad_out[:, 0, cols].unsqueeze(1).to_broadcast([SAMPLES, FRAMES, N_TILE]),
                    )
        for c in range(PASSES):
            load_ctx(c, 1)

        stack.enter_context(tc.manual_schedule())

        def passes(k, order):
            for n, c in enumerate(order):
                patch_pass(accs[k], tiles[k][0], tiles[k][1], c, n == 0, n == len(order) - 1)

        def one_pass(ks, c, start, stop):
            for k in ks:
                patch_pass(accs[k], tiles[k][0], tiles[k][1], c, start, stop)

        products = {}

        def class_mm(k):
            products[k] = class_part(tiles[k][0], tiles[k][1])

        def class_ev(k):
            class_out(products[k], tiles[k][0], tiles[k][1])

        def class_of(k):
            class_mm(k)
            class_ev(k)

        def done(k):
            finish(accs[k], tiles[k][0], tiles[k][1])

        def open_next(n):
            for unused in range(n):
                accs[len(accs)] = open_tile(len(accs))

        def quantise_quarter(grouped, c, first):
            cols = slice(N_TILE + first, N_TILE + first + N_TILE // 2)
            nc.vector.quantize_mx(
                out=ctx_codes[:, c, cols].bitcast(E4M3_X4),
                scales=ctx_scales[:, c, cols],
                in_=grouped[:].rearrange("q w j -> q (w j)"),
            )

        def empty_beside(k):
            patch_sum = spare_pool.tile([M_TILE, N_TILE], F32)
            nc.scalar.copy(out=patch_sum[:], in_=accs[k][:])
            return patch_sum

        def add_beside(patch_sum, k):
            m, h = tiles[k]
            cols = slice(h * N_TILE, (h + 1) * N_TILE)
            nc.gpsimd.tensor_tensor(
                out=result[m][:, cols], in0=patch_sum[:], in1=result[m][:, cols], op=mybir.AluOpType.add
            )

        def store(k):
            m, h = tiles[k]
            rows = slice(m * M_TILE, (m + 1) * M_TILE)
            cols = slice(h * N_TILE, (h + 1) * N_TILE)
            nc.sync.dma_start(out=out[rows, cols], in_=result[m][:, cols])

        accs = {}
        for k in (0, 2, 4, 1, 3, 5):
            accs[k] = open_tile(k)
        for c in range(PASSES):
            ctx_grouped = regroup_ctx(nc.scalar.copy, c, 0)
            left = regroup_grad(nc.vector.tensor_copy, c, 0)
            right = regroup_grad(nc.vector.tensor_copy, c, 1)
            quantise_grad(left, c, 0)
            if c < PASSES - 1:
                quantise_grad(right, c, 1)
            quantise_ctx(ctx_grouped, c, 0)
            for k in range(sum(CLASS_EARLY[0:c]), sum(CLASS_EARLY[0 : c + 1])):
                class_of(k)
            if c < PASSES - 1:
                one_pass(range(WAVE), c, c == 0, False)
            else:
                one_pass(range(0, WAVE, HALVES), c, False, True)
                quantise_grad(right, c, 1)
                one_pass(range(1, WAVE, HALVES), c, False, True)

        HALF = N_TILE // 2
        x0 = late_pool.tile([P, N_TILE, SLOTS], BF16, align_bytes=64, name="late")
        regroup(nc.scalar.copy, x0[:], ctx_raw[0][1][:])
        x1 = stage_pool.tile([P, N_TILE, SLOTS], BF16, align_bytes=64, name="grouped")
        pool_copy(out=x1[:], in_=ctx_raw[1][1][:].rearrange("q j w -> q w j"))
        x2a = stage_pool.tile([P, HALF, SLOTS], BF16, align_bytes=64, name="grouped")
        regroup(nc.scalar.copy, x2a[:], ctx_raw[2][1][:, :, 0:HALF])
        for k in (0, 2, 4):
            done(k)
        open_next(2)
        passes(6, [0, 1, 2])
        passes(7, [0, 1, 2])
        class_mm(9)
        class_mm(10)
        done(1)
        quantise_ctx(x0, 0, 1)
        x2b = late_pool.tile([P, HALF, SLOTS], BF16, align_bytes=64, name="late")
        pool_copy(out=x2b[:], in_=ctx_raw[2][1][:, :, HALF:N_TILE].rearrange("q j w -> q w j"))
        class_ev(9)
        class_ev(10)
        for k in (3, 5):
            done(k)
        open_next(4)
        one_pass(range(8, 10), 0, True, False)
        class_of(11)
        one_pass(range(10, 11), 0, True, False)
        class_of(12)
        one_pass(range(11, 12), 0, True, False)
        class_of(13)
        quantise_ctx(x1, 1, 1)
        one_pass(range(8, 12), 1, False, False)
        quantise_quarter(x2a, 2, 0)
        one_pass(range(8, 12), 2, False, True)
        quantise_quarter(x2b, 2, HALF)
        s10 = empty_beside(10)
        add_beside(s10, 10)
        s11 = empty_beside(11)
        add_beside(s11, 11)
        class_of(14)
        done(6)
        done(7)
        open_next(2)
        passes(12, [0, 1, 2])
        done(8)
        class_of(15)
        passes(13, [0, 1, 2])
        done(9)
        open_next(1)
        passes(14, [0, 1, 2])
        store(10)
        done(12)
        open_next(1)
        passes(15, [0, 1, 2])
        store(11)
        done(13)
        done(14)
        done(15)
